import numpy as np
import ml_dtypes


def mxq(x, axis, fmt="e4m3"):
    dtype, down = {"e4m3": (ml_dtypes.float8_e4m3fn, 7), "e5m2": (ml_dtypes.float8_e5m2, 14)}[fmt]
    v = np.moveaxis(np.asarray(x, np.float32).astype(ml_dtypes.bfloat16).astype(np.float64), axis, -1)
    blocks = v.reshape(v.shape[:-1] + (-1, 32))
    amax = np.abs(blocks).max(-1, keepdims=True)
    byte = np.maximum(np.where(amax > 0, np.frexp(amax)[1] - 1 + 127, 0) - down, 1)
    scale = np.exp2(byte - 127.0)
    codes = (blocks / scale).astype(np.float32).astype(dtype).astype(np.float64)
    return np.moveaxis((codes * scale).reshape(v.shape), -1, axis)


WIDE = False


def mx_kscale(k):
    if not WIDE:
        return np.ones(k)
    levels = np.array([10, -10, 5, -5, 0])
    a = np.random.permutation(np.resize(levels, k // 512 * 4)).reshape(k // 512, 4)
    idx = np.arange(k)
    return np.exp2(a[idx // 512, idx % 128 // 32])


BF16 = ml_dtypes.bfloat16


def bf(x):
    return np.asarray(x, np.float32).astype(BF16)


def f64(x):
    return np.asarray(x).astype(np.float64)


E2M1 = np.array([0.0, 0.5, 1.0, 1.5, 2.0, 3.0, 4.0, 6.0, -0.0, -0.5, -1.0, -1.5, -2.0, -3.0, -4.0, -6.0])


def pack_weight(w, fmt):
    k, n = w.shape
    w = f64(bf(w)).reshape(k // 32, 32, n)
    amax = np.abs(w).max(1)
    if fmt == "e4m3":
        byte = np.frexp(amax)[1] - 1 + 127 - 7
    else:
        mant, ex = np.frexp(amax / 6.0)
        byte = np.where(mant > 0.5, ex, ex - 1) + 127
    byte = np.clip(np.where(amax > 0, byte, 1), 1, 254)
    scaled = (w * np.exp2(127.0 - byte)[:, None, :]).reshape(k, n).astype(np.float32)
    by_word = np.ascontiguousarray(scaled.reshape(k // 512, 128, 4, n).transpose(0, 1, 3, 2))
    if fmt == "e4m3":
        words = by_word.astype(ml_dtypes.float8_e4m3fn).view(np.uint8)
    else:
        c = by_word.astype(ml_dtypes.float4_e2m1fn).view(np.uint8) & 0xF
        words = c[..., 0::2] | (c[..., 1::2] << 4)
    return np.ascontiguousarray(words), np.ascontiguousarray(byte.astype(np.uint8).reshape(k // 512, 16, n))


def unpack_weight(words, scales, fmt):
    g, p, n, _ = words.shape
    if fmt == "e4m3":
        vals = np.ascontiguousarray(words).view(ml_dtypes.float8_e4m3fn).astype(np.float64)
    else:
        nib = np.empty((g, p, n, 4), np.uint8)
        nib[..., 0::2] = words & 0xF
        nib[..., 1::2] = words >> 4
        vals = E2M1[nib]
    vals = vals * np.repeat(np.exp2(scales.astype(np.float64) - 127.0), 8, axis=1)[..., None]
    return vals.transpose(0, 1, 3, 2).reshape(g * 512, n)


B, CIN, CO, H, W, G, KT, KF = 1, 2048, 2048, 8, 16, 8, 3, 3
CG = CO // G
HALF = CO // 2
WIN = KT * KF
FMT = "e4m3"
A = np.sqrt(1.5) / (2.0 * CG) ** 0.25


def unfold(t):
    wins = [t[:, :, i:i + H, j:j + W] for i in range(KT) for j in range(KF)]
    return np.stack(wins, axis=-1).reshape(B, CO, H, W, KT, KF)


def setup_inputs():
    s = mx_kscale(CIN)
    x = bf(np.random.standard_normal((B, CIN, H, W)) * s[None, :, None, None])
    Wq_words, Wq_scales = pack_weight((np.random.standard_normal((CO, CIN)) * A / np.sqrt(CIN) / s[None, :]).T, FMT)
    Wk_words, Wk_scales = pack_weight((np.random.standard_normal((CO, CIN)) * A / np.sqrt(CIN) / s[None, :]).T, FMT)
    Wv_words, Wv_scales = pack_weight((np.random.standard_normal((CO, CIN)) / np.sqrt(CIN) / s[None, :]).T, FMT)
    rel_t = bf(np.random.standard_normal((HALF, KT)) * A)
    rel_f = bf(np.random.standard_normal((HALF, KF)) * A)
    return {
        "x": x,
        "Wq_words": Wq_words,
        "Wq_scales": Wq_scales,
        "Wk_words": Wk_words,
        "Wk_scales": Wk_scales,
        "Wv_words": Wv_words,
        "Wv_scales": Wv_scales,
        "rel_t": rel_t,
        "rel_f": rel_f,
    }


def reference(x, Wq_words, Wq_scales, Wk_words, Wk_scales, Wv_words, Wv_scales, rel_t, rel_f):
    pt, pf = (KT - 1) // 2, (KF - 1) // 2
    xq = mxq(f64(x).reshape(B, CIN, H * W), 1, "e4m3")
    q = (unpack_weight(Wq_words, Wq_scales, FMT).T @ xq).reshape(B, CO, H, W)
    k = (unpack_weight(Wk_words, Wk_scales, FMT).T @ xq).reshape(B, CO, H, W)
    v = (unpack_weight(Wv_words, Wv_scales, FMT).T @ xq).reshape(B, CO, H, W)
    pad = ((0, 0), (0, 0), (pt, pt), (pf, pf))
    kw = unfold(np.pad(k, pad))
    vw = unfold(np.pad(v, pad))
    kw = np.concatenate([
        kw[:, :HALF] + f64(rel_t)[None, :, None, None, :, None],
        kw[:, HALF:] + f64(rel_f)[None, :, None, None, None, :],
    ], axis=1)
    kw = kw.reshape(B, G, CG, H, W, WIN)
    vw = vw.reshape(B, G, CG, H, W, WIN)
    qg = q.reshape(B, G, CG, H, W, 1)
    energy = np.sum(qg * kw, axis=2)
    e = np.exp(energy - energy.max(-1, keepdims=True))
    attn = e / e.sum(-1, keepdims=True)
    out = np.sum(attn[:, :, None] * vw, axis=-1)
    return out.reshape(B, CO, H, W), attn

@@ -1,0 +1,496 @@
+from contextlib import ExitStack
+
+import concourse.mybir as mybir
+from concourse.masks import make_identity
+
+F32 = mybir.dt.float32
+BF16 = mybir.dt.bfloat16
+I32 = mybir.dt.int32
+U32 = mybir.dt.uint32
+U8 = mybir.dt.uint8
+FP8X4 = mybir.dt.float8_e4m3fn_x4
+ALU = mybir.AluOpType
+ACT = mybir.ActivationFunctionType
+AX = mybir.AxisListType
+
+P = 128
+KG = 4
+CO = 2048
+CHUNK = 512
+KR = 136
+NEG = -1.0e30
+V_CHUNKS = ((0,4),(4,4),(8,4),(12,4))
+
+FLOPS = 3 * 2 * 2048 * 2048 * 128 + 2 * 2 * 2048 * 128 * 9
+
+
+def tile_mutliheadattention2d_w_kernel(
+    tc, x, Wq_words, Wq_scales, Wk_words, Wk_scales, Wv_words, Wv_scales, rel_t, rel_f, out_0, out_1
+):
+    nc = tc.nc
+    with ExitStack() as ctx:
+        keep = ctx.enter_context(tc.tile_pool(name="keep", bufs=1))
+        work = ctx.enter_context(tc.tile_pool(name="work", bufs=2))
+        ps_acc = ctx.enter_context(tc.psum_pool(name="ps_acc", bufs=2))
+        ps_s = ctx.enter_context(tc.psum_pool(name="ps_s", bufs=2))
+        ps_tr = ctx.enter_context(tc.psum_pool(name="ps_tr", bufs=2))
+        ps_pv = ctx.enter_context(tc.psum_pool(name="ps_pv", bufs=2))
+        ctx.enter_context(tc.manual_schedule())
+
+        planes = keep.tile([P, 3, CO], U8, name="planes", align_bytes=64)
+        nc.vector.memset(planes[:].bitcast(I32), 0)
+
+        x_raw = keep.tile([P, KG, 4 * P], BF16, name="x_raw")
+        nc.sync.dma_start(out=x_raw[:], in_=x[0].rearrange("(g p t) h w -> p g (t h w)", p=P, t=4))
+
+        z = keep.tile([P, 3 * P], BF16, name="z")
+        nc.vector.memset(z[:], 0.0)
+        nc.scalar.dma_start(out=z[0:8, :], in_=rel_t.rearrange("(m p) n -> m (p n)", p=P))
+        nc.scalar.dma_start(out=z[8:16, :], in_=rel_f.rearrange("(m p) n -> m (p n)", p=P))
+
+        def load_scales(s, sc):
+            for quad in range(4):
+                nc.sync.dma_start(
+                    out=planes[32 * quad : 32 * quad + 16, s, :].bitcast(I32),
+                    in_=sc[:, 4 * quad : 4 * quad + 4, :].bitcast(I32),
+                )
+
+        wq = keep.tile([P, KG, CO], I32, name="wq", align_bytes=64)
+        wk = keep.tile([P, KG, CO], I32, name="wk", align_bytes=64)
+        wv = keep.tile([P, KG, CO], I32, name="wv", align_bytes=64)
+
+        def load_words(dst, src, lo, hi):
+            nc.sync.dma_start(
+                out=dst[:, :, lo:hi],
+                in_=src.rearrange("g p n t -> p g (n t)")[:, :, 4 * lo : 4 * hi].bitcast(I32),
+            )
+
+        load_scales(0, Wq_scales)
+        load_words(wq, Wq_words, 0, 512)
+        load_scales(1, Wk_scales)
+        load_words(wk, Wk_words, 0, 512)
+        load_words(wq, Wq_words, 512, 1024)
+        load_words(wk, Wk_words, 512, 1024)
+        load_words(wq, Wq_words, 1024, 1536)
+        load_words(wk, Wk_words, 1024, 1536)
+        load_scales(2, Wv_scales)
+        load_words(wq, Wq_words, 1536, 2048)
+        load_words(wk, Wk_words, 1536, 2048)
+        load_words(wv, Wv_words, 0, 512)
+        load_words(wv, Wv_words, 512, 1024)
+        load_words(wv, Wv_words, 1024, 1536)
+        load_words(wv, Wv_words, 1536, 2048)
+
+        warm = keep.tile([P, 1], F32, name="warm")
+        nc.vector.memset(warm[:], 0.0)
+        nc.scalar.activation(out=warm[:], in_=warm[:], func=ACT.Exp)
+
+        flag_specs = (
+            ("rot_h", [P, 6], [[-16, 6]], 128, 0x30),
+            ("rot_w", [P, 6], [[-1, 6]], 128, 0x3),
+            ("sel_h", [P, 4, 4], [[-16, 4], [16, 4]], 112, 0x30),
+            ("sel_w", [P, 4, 4], [[-1, 4], [1, 4]], 127, 0x3),
+        )
+        raw = {}
+        for name, shape, pattern, base, bits in flag_specs:
+            raw[name] = keep.tile(shape, I32, name="i_" + name)
+            nc.gpsimd.iota(raw[name][:], pattern=pattern, base=base, channel_multiplier=1)
+        i_p = keep.tile([P, 1], I32, name="i_p")
+        nc.gpsimd.iota(i_p[:], pattern=[[0, 1]], base=0, channel_multiplier=1)
+        ident = keep.tile([P, P], F32, name="ident")
+        make_identity(nc, ident[:])
+        w_pat = [[0, 4], [1, 4], [0, 2], [4, 4]]
+        h_pat = [[1, 4], [0, 4], [4, 2], [0, 4]]
+        i_wp = keep.tile([P, P], I32, name="i_wp")
+        nc.gpsimd.iota(i_wp[:], pattern=w_pat, base=1, channel_multiplier=0)
+        i_wm = keep.tile([P, P], I32, name="i_wm")
+        nc.gpsimd.iota(i_wm[:], pattern=w_pat, base=-1, channel_multiplier=0)
+        i_hp = keep.tile([P, P], I32, name="i_hp")
+        nc.gpsimd.iota(i_hp[:], pattern=h_pat, base=1, channel_multiplier=0)
+        i_hm = keep.tile([P, P], I32, name="i_hm")
+        nc.gpsimd.iota(i_hm[:], pattern=h_pat, base=-1, channel_multiplier=0)
+
+        kr = keep.tile([P, 16, KR], F32, name="kr")
+        nc.vector.memset(kr[:, :, P + 3 : KR], 0.0)
+        flags = {}
+        for name, shape, pattern, base, bits in flag_specs:
+            nc.vector.tensor_single_scalar(out=raw[name][:], in_=raw[name][:], scalar=bits, op=ALU.bitwise_and)
+        i_pw = keep.tile([P, 1], I32, name="i_pw")
+        nc.vector.tensor_single_scalar(out=i_pw[:], in_=i_p[:], scalar=15, op=ALU.bitwise_and)
+        i_ph = keep.tile([P, 1], I32, name="i_ph")
+        nc.vector.tensor_single_scalar(out=i_ph[:], in_=i_p[:], scalar=4, op=ALU.logical_shift_right)
+        for name, shape, pattern, base, bits in flag_specs:
+            flags[name] = keep.tile(shape, F32, name=name)
+            nc.vector.tensor_single_scalar(out=flags[name][:], in_=raw[name][:], scalar=0, op=ALU.is_equal)
+        rot_h, rot_w, sel_h, sel_w = flags["rot_h"], flags["rot_w"], flags["sel_h"], flags["sel_w"]
+        pw = keep.tile([P, 1], F32, name="pw")
+        nc.vector.tensor_copy(out=pw[:], in_=i_pw[:])
+        ph = keep.tile([P, 1], F32, name="ph")
+        nc.vector.tensor_copy(out=ph[:], in_=i_ph[:])
+        vm = keep.tile([P, 4, 4], F32, name="vm")
+        nc.vector.tensor_tensor(
+            out=vm[:],
+            in0=rot_h[:, 2:6].unsqueeze(2).to_broadcast([P, 4, 4]),
+            in1=rot_w[:, 2:6].unsqueeze(1).to_broadcast([P, 4, 4]),
+            op=ALU.max,
+        )
+        zc = keep.tile([P, 3, P], F32, name="zc")
+        nc.vector.tensor_copy(out=zc[:], in_=z[:].rearrange("q (p n) -> q n p", n=3))
+        nc.vector.tensor_single_scalar(out=vm[:], in_=vm[:], scalar=NEG, op=ALU.mult)
+
+        grouped = keep.tile([P, KG, P, 4], BF16, name="grouped", align_bytes=64)
+        nc.vector.tensor_copy(out=grouped[:], in_=x_raw[:].rearrange("p g (t n) -> p g n t", t=4))
+        xc = keep.tile([P, KG * P], U32, name="xc", align_bytes=64)
+        xs = keep.tile([P, KG * P], U8, name="xs", align_bytes=64)
+        grouped_p = keep.tile([P, KG, P, 4], BF16, name="grouped_p", align_bytes=64)
+        src_w = grouped[:].bitcast(F32).rearrange("p g (hh hl wh wl) e -> p hh hl g wl wh e", hh=2, hl=4, wh=4)
+        dst_w = grouped_p[:].bitcast(F32).rearrange("p g (hl wl hh wh) e -> p hl hh g wl wh e", hl=4, wl=4, hh=2)
+        nc.vector.tensor_copy(out=dst_w[:, 0, 0], in_=src_w[:, 0, 0])
+        nc.vector.tensor_copy(out=dst_w[:, 0, 1], in_=src_w[:, 1, 0])
+        nc.vector.quantize_mx(
+            out=xc[:].bitcast(FP8X4), scales=xs[:], in_=grouped[:].rearrange("p g n t -> p (g n t)")
+        )
+        for hl in range(1, 4):
+            for hh in range(2):
+                nc.vector.tensor_copy(out=dst_w[:, hl, hh], in_=src_w[:, hh, hl])
+        band = keep.tile([P, P], F32, name="band")
+        nc.vector.tensor_scalar(out=band[:], in0=i_wp[:], scalar1=pw[:], scalar2=None, op0=ALU.is_ge)
+        xc_p = keep.tile([P, KG * P], U32, name="xc_p", align_bytes=64)
+        xs_p = keep.tile([P, KG * P], U8, name="xs_p", align_bytes=64)
+        nc.vector.quantize_mx(
+            out=xc_p[:].bitcast(FP8X4), scales=xs_p[:], in_=grouped_p[:].rearrange("p g n t -> p (g n t)")
+        )
+        for table, mine, op in ((i_wm, pw, ALU.is_le), (i_hp, ph, ALU.is_ge), (i_hm, ph, ALU.is_le)):
+            nc.vector.scalar_tensor_tensor(
+                out=band[:], in0=table[:], scalar=mine[:], in1=band[:], op0=op, op1=ALU.mult
+            )
+
+        q_sb = keep.tile([P, 16, P], F32, name="q_sb")
+        v_sb = keep.tile([P, CO], F32, name="v_sb")
+        o_sb = keep.tile([P, 16, P], F32, name="o_sb")
+        pt = keep.tile([P, 8, P], F32, name="pt")
+        ca = keep.tile([P, 8, 4, 4], F32, name="ca")
+        pd = keep.tile([P, 8, 16, 8], F32, name="pd")
+        a_sb = keep.tile([P, 8, 3, 3], F32, name="a_sb")
+        out_view = out_0[0].rearrange("(m p) h w -> p m (h w)", p=P)
+        live = {}
+
+        def rel_mm():
+            rel_ps = ps_tr.tile([P, 3, P], F32, tag="tr")
+            for n in range(3):
+                nc.tensor.transpose(out=rel_ps[:, n, :], in_=zc[:, n, :], identity=ident[:])
+            live["rel"] = rel_ps
+
+        def rel_cp():
+            nc.vector.tensor_copy(out=kr[:, :, P : P + 3], in_=live["rel"][:, :, 0:16].rearrange("p n m -> p m n"))
+
+        def project(words, s, c, codes, code_scales):
+            acc = ps_acc.tile([P, 4, P], F32, tag="acc")
+            for j in range(4):
+                cols = slice(P * (4 * c + j), P * (4 * c + j + 1))
+                for g in range(KG):
+                    nc.tensor.matmul_mx(
+                        out=acc[:, j, :],
+                        lhsT=words[:, g, cols].bitcast(FP8X4),
+                        lhsT_scale=planes[4 * g : P, s, cols],
+                        rhs=codes[:, P * g : P * (g + 1)].bitcast(FP8X4),
+                        rhs_scale=code_scales[:, P * g : P * (g + 1)],
+                        start=(g == 0),
+                        stop=(g == KG - 1),
+                    )
+            return acc
+
+        def q_mm(c):
+            live["q", c] = project(wq, 0, c, xc, xs)
+
+        def q_cp(c):
+            nc.scalar.copy(out=q_sb[:, 4 * c : 4 * c + 4, :], in_=live["q", c][:])
+
+        def k_mm(c):
+            live["k", c] = project(wk, 1, c, xc_p, xs_p)
+
+        def k_cp(c):
+            nc.vector.tensor_copy(out=kr[:, 4 * c : 4 * c + 4, 0:P], in_=live["k", c][:])
+
+        def s_mm(c):
+            s_ps = ps_s.tile([P, 2, P + 4], F32, tag="s")
+            for gl in range(2):
+                for s2 in range(2):
+                    m = 4 * c + 2 * gl + s2
+                    nc.tensor.matmul(
+                        out=s_ps[:, gl, :], lhsT=q_sb[:, m, :], rhs=kr[:, m, 0 : P + 4], start=(s2 == 0), stop=(s2 == 1)
+                    )
+            live["s", c] = s_ps
+
+        def mask(c):
+            sm = work.tile([P, 2, 16, 8], F32, tag="sm")
+            nc.vector.tensor_tensor(
+                out=sm[:].rearrange("p g c r -> p g (c r)"),
+                in0=live["s", c][:, :, 0:P],
+                in1=band[:].unsqueeze(1).to_broadcast([P, 2, P]),
+                op=ALU.mult,
+            )
+            live["sm", c] = sm
+
+        def rsel(c):
+            picked = work.tile([P, 2, 4, 4], F32, tag="picked")
+            nc.vector.tensor_tensor(
+                out=picked[:],
+                in0=live["s", c][:, :, P : P + 4].unsqueeze(2).to_broadcast([P, 2, 4, 4]),
+                in1=(sel_h if c < 2 else sel_w)[:].unsqueeze(1).to_broadcast([P, 2, 4, 4]),
+                op=ALU.mult,
+            )
+            live["picked", c] = picked
+
+        def red(c):
+            e = work.tile([P, 2, 16], F32, tag="e")
+            nc.vector.tensor_reduce(out=e[:], in_=live["sm", c][:], axis=AX.X, op=ALU.add)
+            live["e", c] = e
+
+        def rc(c):
+            r_cls = work.tile([P, 2, 4], F32, tag="r_cls")
+            nc.vector.tensor_reduce(out=r_cls[:], in_=live["picked", c][:], axis=AX.X, op=ALU.add)
+            live["r_cls", c] = r_cls
+
+        def rv(c):
+            r_all = work.tile([P, 2, 4, 4], F32, tag="r_all")
+            nc.vector.tensor_tensor(
+                out=r_all[:],
+                in0=vm[:].unsqueeze(1).to_broadcast([P, 2, 4, 4]),
+                in1=live["r_cls", c][:].unsqueeze(3 if c < 2 else 2).to_broadcast([P, 2, 4, 4]),
+                op=ALU.add,
+            )
+            live["r_all", c] = r_all
+
+        def eadd(c):
+            e = live["e", c]
+            nc.vector.tensor_tensor(
+                out=e[:], in0=e[:], in1=live["r_all", c][:].rearrange("p g a b -> p g (a b)"), op=ALU.add
+            )
+
+        def negmx(c):
+            neg_max = work.tile([P, 2], F32, tag="neg_max")
+            nc.vector.tensor_reduce(out=neg_max[:], in_=live["e", c][:], axis=AX.X, op=ALU.max, negate=True)
+            live["neg_max", c] = neg_max
+
+        def exp(c):
+            e = live["e", c]
+            den = work.tile([P, 2], F32, tag="den")
+            for gl in range(2):
+                nc.scalar.activation(
+                    out=e[:, gl, :],
+                    in_=e[:, gl, :],
+                    func=ACT.Exp,
+                    bias=live["neg_max", c][:, gl : gl + 1],
+                    scale=1.0,
+                    accum_out=den[:, gl : gl + 1],
+                )
+            live["den", c] = den
+
+        def recip(c):
+            nc.vector.reciprocal(out=live["den", c][:], in_=live["den", c][:])
+
+        def canorm(c):
+            nc.vector.tensor_tensor(
+                out=ca[:, 2 * c : 2 * c + 2].rearrange("p g a b -> p g (a b)"),
+                in0=live["e", c][:],
+                in1=live["den", c][:].unsqueeze(2).to_broadcast([P, 2, 16]),
+                op=ALU.mult,
+            )
+
+        def pdense(c):
+            nc.vector.tensor_tensor(
+                out=pd[:, 2 * c : 2 * c + 2],
+                in0=ca[:, 2 * c : 2 * c + 2].rearrange("p g a b -> p g (a b)").unsqueeze(3).to_broadcast([P, 2, 16, 8]),
+                in1=band[:].rearrange("p (c r) -> p c r", r=8).unsqueeze(1).to_broadcast([P, 2, 16, 8]),
+                op=ALU.mult,
+            )
+
+        def t_mm(c):
+            tr_ps = ps_tr.tile([P, 2, P], F32, tag="tr")
+            for gl in range(2):
+                nc.tensor.transpose(
+                    out=tr_ps[:, gl, :], in_=pd[:, 2 * c + gl].rearrange("p c r -> p (c r)"), identity=ident[:]
+                )
+            live["tr", c] = tr_ps
+
+        def t_cp(c):
+            nc.scalar.copy(out=pt[:, 2 * c : 2 * c + 2, :], in_=live["tr", c][:])
+
+        def v_mm(i):
+            m0, n_tiles = V_CHUNKS[i]
+            vacc = ps_acc.tile([P, P * n_tiles], F32, tag="acc")
+            cols = slice(P * m0, P * (m0 + n_tiles))
+            for g in range(KG):
+                nc.tensor.matmul_mx(
+                    out=vacc[:],
+                    lhsT=xc_p[:, P * g : P * (g + 1)].bitcast(FP8X4),
+                    lhsT_scale=xs_p[:, P * g : P * (g + 1)],
+                    rhs=wv[:, g, cols].bitcast(FP8X4),
+                    rhs_scale=planes[4 * g : P, 2, cols],
+                    start=(g == 0),
+                    stop=(g == KG - 1),
+                )
+            live["v", i] = vacc
+
+        def v_cp(i):
+            m0, n_tiles = V_CHUNKS[i]
+            nc.scalar.copy(out=v_sb[:, P * m0 : P * (m0 + n_tiles)], in_=live["v", i][:])
+
+        def p_mm(i):
+            m0, n_tiles = V_CHUNKS[i]
+            pv = ps_pv.tile([P, n_tiles, P], F32, tag="pv")
+            for j in range(n_tiles):
+                m = m0 + j
+                nc.tensor.matmul(
+                    out=pv[:, j, :], lhsT=v_sb[:, P * m : P * (m + 1)], rhs=pt[:, m // 2, :], start=True, stop=True
+                )
+            live["pv", i] = pv
+
+        def o_cp(i):
+            m0, n_tiles = V_CHUNKS[i]
+            nc.vector.tensor_copy(out=o_sb[:, m0 : m0 + n_tiles, :], in_=live["pv", i][:])
+            nc.sync.dma_start(out=out_view[:, m0 : m0 + n_tiles, :], in_=o_sb[:, m0 : m0 + n_tiles, :])
+
+        def w1_(half):
+            by_a = work.tile([P, 4, 3, 4, 4], F32, tag="by_a")
+            for i in range(3):
+                nc.vector.tensor_tensor(
+                    out=by_a[:, :, i],
+                    in0=ca[:, 4 * half : 4 * half + 4].rearrange("p g a b -> p g b a"),
+                    in1=sel_h[:, :, i].unsqueeze(1).unsqueeze(1).to_broadcast([P, 4, 4, 4]),
+                    op=ALU.mult,
+                )
+            live["by_a", half] = by_a
+
+        def w2_(half):
+            rows = work.tile([P, 12, 4], F32, tag="rows")
+            nc.vector.tensor_reduce(
+                out=rows[:].rearrange("p r b -> p (r b)"),
+                in_=live["by_a", half][:].rearrange("p g i b a -> p (g i b) a"),
+                axis=AX.X,
+                op=ALU.add,
+            )
+            live["rows", half] = rows
+
+        def w3_(half):
+            by_b = work.tile([P, 12, 3, 4], F32, tag="by_b")
+            nc.vector.tensor_tensor(
+                out=by_b[:],
+                in0=live["rows", half][:].unsqueeze(2).to_broadcast([P, 12, 3, 4]),
+                in1=sel_w[:, :, 0:3].rearrange("p b j -> p j b").unsqueeze(1).to_broadcast([P, 12, 3, 4]),
+                op=ALU.mult,
+            )
+            live["by_b", half] = by_b
+
+        def w4_(half):
+            g0 = 4 * half
+            nc.vector.tensor_reduce(
+                out=a_sb[:, g0 : g0 + 4].rearrange("p g i j -> p (g i j)"),
+                in_=live["by_b", half][:].rearrange("p r j b -> p (r j) b"),
+                axis=AX.X,
+                op=ALU.add,
+            )
+            nc.sync.dma_start(
+                out=out_1[0, g0 : g0 + 4].rearrange("g h w n -> (h w) g n"),
+                in_=a_sb[:, g0 : g0 + 4].rearrange("p g i j -> p g (i j)"),
+            )
+
+        rel_mm()
+        rel_cp()
+        q_mm(0)
+        q_cp(0)
+        k_mm(0)
+        k_cp(0)
+        q_mm(1)
+        s_mm(0)
+        q_cp(1)
+        k_mm(1)
+        mask(0)
+        rsel(0)
+        red(0)
+        rc(0)
+        k_cp(1)
+        rv(0)
+        q_mm(2)
+        eadd(0)
+        negmx(0)
+        exp(0)
+        s_mm(1)
+        q_cp(2)
+        recip(0)
+        canorm(0)
+        k_mm(2)
+        pdense(0)
+        mask(1)
+        rsel(1)
+        red(1)
+        t_mm(0)
+        rc(1)
+        k_cp(2)
+        t_cp(0)
+        rv(1)
+        q_mm(3)
+        eadd(1)
+        negmx(1)
+        exp(1)
+        s_mm(2)
+        recip(1)
+        q_cp(3)
+        canorm(1)
+        pdense(1)
+        k_mm(3)
+        w1_(0)
+        mask(2)
+        rsel(2)
+        w2_(0)
+        red(2)
+        t_mm(1)
+        rc(2)
+        w3_(0)
+        k_cp(3)
+        t_cp(1)
+        v_mm(0)
+        rv(2)
+        w4_(0)
+        eadd(2)
+        negmx(2)
+        exp(2)
+        s_mm(3)
+        v_cp(0)
+        recip(2)
+        canorm(2)
+        v_mm(1)
+        pdense(2)
+        mask(3)
+        rsel(3)
+        red(3)
+        t_mm(2)
+        rc(3)
+        p_mm(0)
+        v_cp(1)
+        rv(3)
+        eadd(3)
+        t_cp(2)
+        negmx(3)
+        exp(3)
+        p_mm(1)
+        o_cp(0)
+        recip(3)
+        v_mm(2)
+        canorm(3)
+        o_cp(1)
+        pdense(3)
+        v_mm(3)
+        w1_(1)
+        v_cp(2)
+        w2_(1)
+        w3_(1)
+        t_mm(3)
+        p_mm(2)
+        v_cp(3)
+        w4_(1)
+        t_cp(3)
+        p_mm(3)
+        o_cp(2)
+        o_cp(3)

@@ -19,7 +19,7 @@ CO = 2048
 CHUNK = 512
 KR = 136
 NEG = -1.0e30
-V_CHUNKS = ((0,4),(4,4),(8,4),(12,4))
+V_CHUNKS = ((0,4),(4,4),(8,4),(12,2),(14,2))
 
 FLOPS = 3 * 2 * 2048 * 2048 * 128 + 2 * 2 * 2048 * 128 * 9
 
@@ -65,6 +65,11 @@ def tile_mutliheadattention2d_w_kernel(
                 in_=src.rearrange("g p n t -> p g (n t)")[:, :, 4 * lo : 4 * hi].bitcast(I32),
             )
 
+        def load_words_g(dst, src, g, lo, hi):
+            nc.sync.dma_start(
+                out=dst[:, g, lo:hi], in_=src[g].rearrange("p n t -> p (n t)")[:, 4 * lo : 4 * hi].bitcast(I32)
+            )
+
         load_scales(0, Wq_scales)
         load_words(wq, Wq_words, 0, 512)
         load_scales(1, Wk_scales)
@@ -75,11 +80,13 @@ def tile_mutliheadattention2d_w_kernel(
         load_words(wk, Wk_words, 1024, 1536)
         load_scales(2, Wv_scales)
         load_words(wq, Wq_words, 1536, 2048)
-        load_words(wk, Wk_words, 1536, 2048)
+        for g in range(KG):
+            load_words_g(wk, Wk_words, g, 1536, 2048)
         load_words(wv, Wv_words, 0, 512)
         load_words(wv, Wv_words, 512, 1024)
         load_words(wv, Wv_words, 1024, 1536)
-        load_words(wv, Wv_words, 1536, 2048)
+        for g in range(KG):
+            load_words_g(wv, Wv_words, g, 1536, 2048)
 
         warm = keep.tile([P, 1], F32, name="warm")
         nc.vector.memset(warm[:], 0.0)
@@ -209,8 +216,24 @@ def tile_mutliheadattention2d_w_kernel(
         def k_mm(c):
             live["k", c] = project(wk, 1, c, xc_p, xs_p)
 
+        def kk_mm(g):
+            if g == 0:
+                acc = ps_acc.tile([P, 4, P], F32, tag="acc")
+                live["k", 3] = acc
+            for j in range(4):
+                cols = slice(P * (12 + j), P * (13 + j))
+                nc.tensor.matmul_mx(
+                    out=live["k", 3][:, j, :],
+                    lhsT=wk[:, g, cols].bitcast(FP8X4),
+                    lhsT_scale=planes[4 * g : P, 1, cols],
+                    rhs=xc_p[:, P * g : P * (g + 1)].bitcast(FP8X4),
+                    rhs_scale=xs_p[:, P * g : P * (g + 1)],
+                    start=(g == 0 and j == 0),
+                    stop=(g == KG - 1 and j == 3),
+                )
+
         def k_cp(c):
-            nc.vector.tensor_copy(out=kr[:, 4 * c : 4 * c + 4, 0:P], in_=live["k", c][:])
+            nc.scalar.copy(out=kr[:, 4 * c : 4 * c + 4, 0:P], in_=live["k", c][:])
 
         def s_mm(c):
             s_ps = ps_s.tile([P, 2, P + 4], F32, tag="s")
@@ -333,13 +356,36 @@ def tile_mutliheadattention2d_w_kernel(
                 )
             live["v", i] = vacc
 
+        def vv_mm(g):
+            for i in (3, 4):
+                m0, n_tiles = V_CHUNKS[i]
+                if g == 0:
+                    vacc = ps_s.tile([P, P * n_tiles], F32, tag="s")
+                    live["v", i] = vacc
+                cols = slice(P * m0, P * (m0 + n_tiles))
+                nc.tensor.matmul_mx(
+                    out=live["v", i][:],
+                    lhsT=xc_p[:, P * g : P * (g + 1)].bitcast(FP8X4),
+                    lhsT_scale=xs_p[:, P * g : P * (g + 1)],
+                    rhs=wv[:, g, cols].bitcast(FP8X4),
+                    rhs_scale=planes[4 * g : P, 2, cols],
+                    start=(g == 0),
+                    stop=(g == KG - 1),
+                )
+
         def v_cp(i):
             m0, n_tiles = V_CHUNKS[i]
-            nc.scalar.copy(out=v_sb[:, P * m0 : P * (m0 + n_tiles)], in_=live["v", i][:])
+            if i == 4:
+                nc.vector.tensor_copy(out=v_sb[:, P * m0 : P * (m0 + n_tiles)], in_=live["v", i][:])
+            else:
+                nc.scalar.copy(out=v_sb[:, P * m0 : P * (m0 + n_tiles)], in_=live["v", i][:])
 
         def p_mm(i):
             m0, n_tiles = V_CHUNKS[i]
-            pv = ps_pv.tile([P, n_tiles, P], F32, tag="pv")
+            if i == 4:
+                pv = ps_tr.tile([P, n_tiles, P], F32, tag="tr")
+            else:
+                pv = ps_pv.tile([P, n_tiles, P], F32, tag="pv")
             for j in range(n_tiles):
                 m = m0 + j
                 nc.tensor.matmul(
@@ -349,7 +395,10 @@ def tile_mutliheadattention2d_w_kernel(
 
         def o_cp(i):
             m0, n_tiles = V_CHUNKS[i]
-            nc.vector.tensor_copy(out=o_sb[:, m0 : m0 + n_tiles, :], in_=live["pv", i][:])
+            if i == 3:
+                nc.scalar.copy(out=o_sb[:, m0 : m0 + n_tiles, :], in_=live["pv", i][:])
+            else:
+                nc.vector.tensor_copy(out=o_sb[:, m0 : m0 + n_tiles, :], in_=live["pv", i][:])
             nc.sync.dma_start(out=out_view[:, m0 : m0 + n_tiles, :], in_=o_sb[:, m0 : m0 + n_tiles, :])
 
         def w1_(half):
@@ -402,95 +451,104 @@ def tile_mutliheadattention2d_w_kernel(
         q_cp(0)
         k_mm(0)
         k_cp(0)
-        q_mm(1)
         s_mm(0)
-        q_cp(1)
-        k_mm(1)
         mask(0)
         rsel(0)
         red(0)
         rc(0)
-        k_cp(1)
         rv(0)
-        q_mm(2)
         eadd(0)
         negmx(0)
+        q_mm(1)
+        q_cp(1)
         exp(0)
+        k_mm(1)
+        k_cp(1)
         s_mm(1)
-        q_cp(2)
         recip(0)
         canorm(0)
-        k_mm(2)
         pdense(0)
         mask(1)
         rsel(1)
         red(1)
-        t_mm(0)
         rc(1)
-        k_cp(2)
-        t_cp(0)
         rv(1)
-        q_mm(3)
         eadd(1)
         negmx(1)
+        q_mm(2)
+        q_cp(2)
         exp(1)
+        k_mm(2)
+        k_cp(2)
+        t_mm(0)
+        t_cp(0)
         s_mm(2)
         recip(1)
-        q_cp(3)
         canorm(1)
         pdense(1)
-        k_mm(3)
         w1_(0)
+        w2_(0)
         mask(2)
         rsel(2)
-        w2_(0)
-        red(2)
-        t_mm(1)
-        rc(2)
         w3_(0)
-        k_cp(3)
-        t_cp(1)
-        v_mm(0)
-        rv(2)
+        red(2)
+        rc(2)
         w4_(0)
+        rv(2)
         eadd(2)
         negmx(2)
+        q_mm(3)
+        q_cp(3)
         exp(2)
+        kk_mm(0)
+        kk_mm(1)
+        kk_mm(2)
+        kk_mm(3)
+        k_cp(3)
+        t_mm(1)
+        t_cp(1)
         s_mm(3)
-        v_cp(0)
         recip(2)
         canorm(2)
-        v_mm(1)
         pdense(2)
         mask(3)
         rsel(3)
         red(3)
-        t_mm(2)
         rc(3)
-        p_mm(0)
-        v_cp(1)
         rv(3)
         eadd(3)
-        t_cp(2)
         negmx(3)
+        v_mm(0)
+        v_cp(0)
         exp(3)
-        p_mm(1)
-        o_cp(0)
+        v_mm(1)
+        v_cp(1)
+        t_mm(2)
+        t_cp(2)
+        p_mm(0)
         recip(3)
-        v_mm(2)
         canorm(3)
-        o_cp(1)
         pdense(3)
-        v_mm(3)
         w1_(1)
-        v_cp(2)
         w2_(1)
+        o_cp(0)
         w3_(1)
-        t_mm(3)
-        p_mm(2)
-        v_cp(3)
         w4_(1)
+        p_mm(1)
+        o_cp(1)
+        v_mm(2)
+        v_cp(2)
+        vv_mm(0)
+        vv_mm(1)
+        vv_mm(2)
+        t_mm(3)
         t_cp(3)
+        vv_mm(3)
+        v_cp(3)
+        v_cp(4)
+        p_mm(2)
         p_mm(3)
         o_cp(2)
+        p_mm(4)
         o_cp(3)
+        o_cp(4)

@@ -38,15 +38,19 @@ def tile_mutliheadattention2d_w_kernel(
         ctx.enter_context(tc.manual_schedule())
 
         planes = keep.tile([P, 3, CO], U8, name="planes", align_bytes=64)
-        nc.vector.memset(planes[:].bitcast(I32), 0)
+        for s in range(3):
+            nc.vector.memset(planes[:, s, :].bitcast(I32), 0)
 
         x_raw = keep.tile([P, KG, 4 * P], BF16, name="x_raw")
         nc.sync.dma_start(out=x_raw[:], in_=x[0].rearrange("(g p t) h w -> p g (t h w)", p=P, t=4))
 
         z = keep.tile([P, 3 * P], BF16, name="z")
-        nc.vector.memset(z[:], 0.0)
+        nc.gpsimd.memset(z[:], 0.0)
+        warm = keep.tile([P, 1], F32, name="warm")
+        nc.gpsimd.memset(warm[:], 0.0)
         nc.scalar.dma_start(out=z[0:8, :], in_=rel_t.rearrange("(m p) n -> m (p n)", p=P))
         nc.scalar.dma_start(out=z[8:16, :], in_=rel_f.rearrange("(m p) n -> m (p n)", p=P))
+        nc.scalar.activation(out=warm[:], in_=warm[:], func=ACT.Exp)
 
         def load_scales(s, sc):
             for quad in range(4):
@@ -88,10 +92,6 @@ def tile_mutliheadattention2d_w_kernel(
         for g in range(KG):
             load_words_g(wv, Wv_words, g, 1536, 2048)
 
-        warm = keep.tile([P, 1], F32, name="warm")
-        nc.vector.memset(warm[:], 0.0)
-        nc.scalar.activation(out=warm[:], in_=warm[:], func=ACT.Exp)
-
         flag_specs = (
             ("rot_h", [P, 6], [[-16, 6]], 128, 0x30),
             ("rot_w", [P, 6], [[-1, 6]], 128, 0x3),
@@ -106,6 +106,7 @@ def tile_mutliheadattention2d_w_kernel(
         nc.gpsimd.iota(i_p[:], pattern=[[0, 1]], base=0, channel_multiplier=1)
         ident = keep.tile([P, P], F32, name="ident")
         make_identity(nc, ident[:])
+        kr = keep.tile([P, 16, KR], F32, name="kr")
         w_pat = [[0, 4], [1, 4], [0, 2], [4, 4]]
         h_pat = [[1, 4], [0, 4], [4, 2], [0, 4]]
         i_wp = keep.tile([P, P], I32, name="i_wp")
@@ -117,7 +118,9 @@ def tile_mutliheadattention2d_w_kernel(
         i_hm = keep.tile([P, P], I32, name="i_hm")
         nc.gpsimd.iota(i_hm[:], pattern=h_pat, base=-1, channel_multiplier=0)
 
-        kr = keep.tile([P, 16, KR], F32, name="kr")
+        zc = keep.tile([P, 3, P], F32, name="zc")
+        nc.scalar.copy(out=zc[:], in_=z[:].rearrange("q (p n) -> q n p", n=3))
+
         nc.vector.memset(kr[:, :, P + 3 : KR], 0.0)
         flags = {}
         for name, shape, pattern, base, bits in flag_specs:
@@ -141,8 +144,6 @@ def tile_mutliheadattention2d_w_kernel(
             in1=rot_w[:, 2:6].unsqueeze(1).to_broadcast([P, 4, 4]),
             op=ALU.max,
         )
-        zc = keep.tile([P, 3, P], F32, name="zc")
-        nc.vector.tensor_copy(out=zc[:], in_=z[:].rearrange("q (p n) -> q n p", n=3))
         nc.vector.tensor_single_scalar(out=vm[:], in_=vm[:], scalar=NEG, op=ALU.mult)
 
         grouped = keep.tile([P, KG, P, 4], BF16, name="grouped", align_bytes=64)

@@ -214,27 +214,38 @@ def tile_mutliheadattention2d_w_kernel(
         def q_cp(c):
             nc.scalar.copy(out=q_sb[:, 4 * c : 4 * c + 4, :], in_=live["q", c][:])
 
+        def k_banks(c):
+            ka = ps_acc.tile([P, 2, P], F32, tag="acc")
+            kb = ps_pv.tile([P, 2, P], F32, tag="pv")
+            live["k", c] = (ka, kb)
+
+        def k_pass(c, j, g, start, stop):
+            cols = slice(P * (4 * c + j), P * (4 * c + j + 1))
+            nc.tensor.matmul_mx(
+                out=live["k", c][j // 2][:, j % 2, :],
+                lhsT=wk[:, g, cols].bitcast(FP8X4),
+                lhsT_scale=planes[4 * g : P, 1, cols],
+                rhs=xc_p[:, P * g : P * (g + 1)].bitcast(FP8X4),
+                rhs_scale=xs_p[:, P * g : P * (g + 1)],
+                start=start,
+                stop=stop,
+            )
+
         def k_mm(c):
-            live["k", c] = project(wk, 1, c, xc_p, xs_p)
+            k_banks(c)
+            for j in range(4):
+                for g in range(KG):
+                    k_pass(c, j, g, g == 0, g == KG - 1)
 
         def kk_mm(g):
             if g == 0:
-                acc = ps_acc.tile([P, 4, P], F32, tag="acc")
-                live["k", 3] = acc
+                k_banks(3)
             for j in range(4):
-                cols = slice(P * (12 + j), P * (13 + j))
-                nc.tensor.matmul_mx(
-                    out=live["k", 3][:, j, :],
-                    lhsT=wk[:, g, cols].bitcast(FP8X4),
-                    lhsT_scale=planes[4 * g : P, 1, cols],
-                    rhs=xc_p[:, P * g : P * (g + 1)].bitcast(FP8X4),
-                    rhs_scale=xs_p[:, P * g : P * (g + 1)],
-                    start=(g == 0 and j == 0),
-                    stop=(g == KG - 1 and j == 3),
-                )
+                k_pass(3, j, g, g == 0 and j % 2 == 0, g == KG - 1 and j % 2 == 1)
 
         def k_cp(c):
-            nc.scalar.copy(out=kr[:, 4 * c : 4 * c + 4, 0:P], in_=live["k", c][:])
+            nc.scalar.copy(out=kr[:, 4 * c : 4 * c + 2, 0:P], in_=live["k", c][0][:])
+            nc.vector.tensor_copy(out=kr[:, 4 * c + 2 : 4 * c + 4, 0:P], in_=live["k", c][1][:])
 
         def s_mm(c):
             s_ps = ps_s.tile([P, 2, P + 4], F32, tag="s")

@@ -543,9 +543,9 @@ def tile_mutliheadattention2d_w_kernel(
         pdense(3)
         w1_(1)
         w2_(1)
-        o_cp(0)
         w3_(1)
         w4_(1)
+        o_cp(0)
         p_mm(1)
         o_cp(1)
         v_mm(2)

from contextlib import ExitStack

import concourse.mybir as mybir
from concourse.masks import make_identity

F32 = mybir.dt.float32
BF16 = mybir.dt.bfloat16
I32 = mybir.dt.int32
U32 = mybir.dt.uint32
U8 = mybir.dt.uint8
FP8X4 = mybir.dt.float8_e4m3fn_x4
ALU = mybir.AluOpType
ACT = mybir.ActivationFunctionType
AX = mybir.AxisListType

P = 128
KG = 4
CO = 2048
CHUNK = 512
KR = 136
NEG = -1.0e30
V_CHUNKS = ((0,4),(4,4),(8,4),(12,2),(14,2))

FLOPS = 3 * 2 * 2048 * 2048 * 128 + 2 * 2 * 2048 * 128 * 9


def tile_mutliheadattention2d_w_kernel(
    tc, x, Wq_words, Wq_scales, Wk_words, Wk_scales, Wv_words, Wv_scales, rel_t, rel_f, out_0, out_1
):
    nc = tc.nc
    with ExitStack() as ctx:
        keep = ctx.enter_context(tc.tile_pool(name="keep", bufs=1))
        work = ctx.enter_context(tc.tile_pool(name="work", bufs=2))
        ps_acc = ctx.enter_context(tc.psum_pool(name="ps_acc", bufs=2))
        ps_s = ctx.enter_context(tc.psum_pool(name="ps_s", bufs=2))
        ps_tr = ctx.enter_context(tc.psum_pool(name="ps_tr", bufs=2))
        ps_pv = ctx.enter_context(tc.psum_pool(name="ps_pv", bufs=2))
        ctx.enter_context(tc.manual_schedule())

        planes = keep.tile([P, 3, CO], U8, name="planes", align_bytes=64)
        for s in range(3):
            nc.vector.memset(planes[:, s, :].bitcast(I32), 0)

        x_raw = keep.tile([P, KG, 4 * P], BF16, name="x_raw")
        nc.sync.dma_start(out=x_raw[:], in_=x[0].rearrange("(g p t) h w -> p g (t h w)", p=P, t=4))

        z = keep.tile([P, 3 * P], BF16, name="z")
        nc.gpsimd.memset(z[:], 0.0)
        warm = keep.tile([P, 1], F32, name="warm")
        nc.gpsimd.memset(warm[:], 0.0)
        nc.scalar.dma_start(out=z[0:8, :], in_=rel_t.rearrange("(m p) n -> m (p n)", p=P))
        nc.scalar.dma_start(out=z[8:16, :], in_=rel_f.rearrange("(m p) n -> m (p n)", p=P))
        nc.scalar.activation(out=warm[:], in_=warm[:], func=ACT.Exp)

        def load_scales(s, sc):
            for quad in range(4):
                nc.sync.dma_start(
                    out=planes[32 * quad : 32 * quad + 16, s, :].bitcast(I32),
                    in_=sc[:, 4 * quad : 4 * quad + 4, :].bitcast(I32),
                )

        wq = keep.tile([P, KG, CO], I32, name="wq", align_bytes=64)
        wk = keep.tile([P, KG, CO], I32, name="wk", align_bytes=64)
        wv = keep.tile([P, KG, CO], I32, name="wv", align_bytes=64)

        def load_words(dst, src, lo, hi):
            nc.sync.dma_start(
                out=dst[:, :, lo:hi],
                in_=src.rearrange("g p n t -> p g (n t)")[:, :, 4 * lo : 4 * hi].bitcast(I32),
            )

        def load_words_g(dst, src, g, lo, hi):
            nc.sync.dma_start(
                out=dst[:, g, lo:hi], in_=src[g].rearrange("p n t -> p (n t)")[:, 4 * lo : 4 * hi].bitcast(I32)
            )

        load_scales(0, Wq_scales)
        load_words(wq, Wq_words, 0, 512)
        load_scales(1, Wk_scales)
        load_words(wk, Wk_words, 0, 512)
        load_words(wq, Wq_words, 512, 1024)
        load_words(wk, Wk_words, 512, 1024)
        load_words(wq, Wq_words, 1024, 1536)
        load_words(wk, Wk_words, 1024, 1536)
        load_scales(2, Wv_scales)
        load_words(wq, Wq_words, 1536, 2048)
        for g in range(KG):
            load_words_g(wk, Wk_words, g, 1536, 2048)
        load_words(wv, Wv_words, 0, 512)
        load_words(wv, Wv_words, 512, 1024)
        load_words(wv, Wv_words, 1024, 1536)
        for g in range(KG):
            load_words_g(wv, Wv_words, g, 1536, 2048)

        flag_specs = (
            ("rot_h", [P, 6], [[-16, 6]], 128, 0x30),
            ("rot_w", [P, 6], [[-1, 6]], 128, 0x3),
            ("sel_h", [P, 4, 4], [[-16, 4], [16, 4]], 112, 0x30),
            ("sel_w", [P, 4, 4], [[-1, 4], [1, 4]], 127, 0x3),
        )
        raw = {}
        for name, shape, pattern, base, bits in flag_specs:
            raw[name] = keep.tile(shape, I32, name="i_" + name)
            nc.gpsimd.iota(raw[name][:], pattern=pattern, base=base, channel_multiplier=1)
        i_p = keep.tile([P, 1], I32, name="i_p")
        nc.gpsimd.iota(i_p[:], pattern=[[0, 1]], base=0, channel_multiplier=1)
        ident = keep.tile([P, P], F32, name="ident")
        make_identity(nc, ident[:])
        kr = keep.tile([P, 16, KR], F32, name="kr")
        w_pat = [[0, 4], [1, 4], [0, 2], [4, 4]]
        h_pat = [[1, 4], [0, 4], [4, 2], [0, 4]]
        i_wp = keep.tile([P, P], I32, name="i_wp")
        nc.gpsimd.iota(i_wp[:], pattern=w_pat, base=1, channel_multiplier=0)
        i_wm = keep.tile([P, P], I32, name="i_wm")
        nc.gpsimd.iota(i_wm[:], pattern=w_pat, base=-1, channel_multiplier=0)
        i_hp = keep.tile([P, P], I32, name="i_hp")
        nc.gpsimd.iota(i_hp[:], pattern=h_pat, base=1, channel_multiplier=0)
        i_hm = keep.tile([P, P], I32, name="i_hm")
        nc.gpsimd.iota(i_hm[:], pattern=h_pat, base=-1, channel_multiplier=0)

        zc = keep.tile([P, 3, P], F32, name="zc")
        nc.scalar.copy(out=zc[:], in_=z[:].rearrange("q (p n) -> q n p", n=3))

        nc.vector.memset(kr[:, :, P + 3 : KR], 0.0)
        flags = {}
        for name, shape, pattern, base, bits in flag_specs:
            nc.vector.tensor_single_scalar(out=raw[name][:], in_=raw[name][:], scalar=bits, op=ALU.bitwise_and)
        i_pw = keep.tile([P, 1], I32, name="i_pw")
        nc.vector.tensor_single_scalar(out=i_pw[:], in_=i_p[:], scalar=15, op=ALU.bitwise_and)
        i_ph = keep.tile([P, 1], I32, name="i_ph")
        nc.vector.tensor_single_scalar(out=i_ph[:], in_=i_p[:], scalar=4, op=ALU.logical_shift_right)
        for name, shape, pattern, base, bits in flag_specs:
            flags[name] = keep.tile(shape, F32, name=name)
            nc.vector.tensor_single_scalar(out=flags[name][:], in_=raw[name][:], scalar=0, op=ALU.is_equal)
        rot_h, rot_w, sel_h, sel_w = flags["rot_h"], flags["rot_w"], flags["sel_h"], flags["sel_w"]
        pw = keep.tile([P, 1], F32, name="pw")
        nc.vector.tensor_copy(out=pw[:], in_=i_pw[:])
        ph = keep.tile([P, 1], F32, name="ph")
        nc.vector.tensor_copy(out=ph[:], in_=i_ph[:])
        vm = keep.tile([P, 4, 4], F32, name="vm")
        nc.vector.tensor_tensor(
            out=vm[:],
            in0=rot_h[:, 2:6].unsqueeze(2).to_broadcast([P, 4, 4]),
            in1=rot_w[:, 2:6].unsqueeze(1).to_broadcast([P, 4, 4]),
            op=ALU.max,
        )
        nc.vector.tensor_single_scalar(out=vm[:], in_=vm[:], scalar=NEG, op=ALU.mult)

        grouped = keep.tile([P, KG, P, 4], BF16, name="grouped", align_bytes=64)
        nc.vector.tensor_copy(out=grouped[:], in_=x_raw[:].rearrange("p g (t n) -> p g n t", t=4))
        xc = keep.tile([P, KG * P], U32, name="xc", align_bytes=64)
        xs = keep.tile([P, KG * P], U8, name="xs", align_bytes=64)
        grouped_p = keep.tile([P, KG, P, 4], BF16, name="grouped_p", align_bytes=64)
        src_w = grouped[:].bitcast(F32).rearrange("p g (hh hl wh wl) e -> p hh hl g wl wh e", hh=2, hl=4, wh=4)
        dst_w = grouped_p[:].bitcast(F32).rearrange("p g (hl wl hh wh) e -> p hl hh g wl wh e", hl=4, wl=4, hh=2)
        nc.vector.tensor_copy(out=dst_w[:, 0, 0], in_=src_w[:, 0, 0])
        nc.vector.tensor_copy(out=dst_w[:, 0, 1], in_=src_w[:, 1, 0])
        nc.vector.quantize_mx(
            out=xc[:].bitcast(FP8X4), scales=xs[:], in_=grouped[:].rearrange("p g n t -> p (g n t)")
        )
        for hl in range(1, 4):
            for hh in range(2):
                nc.vector.tensor_copy(out=dst_w[:, hl, hh], in_=src_w[:, hh, hl])
        band = keep.tile([P, P], F32, name="band")
        nc.vector.tensor_scalar(out=band[:], in0=i_wp[:], scalar1=pw[:], scalar2=None, op0=ALU.is_ge)
        xc_p = keep.tile([P, KG * P], U32, name="xc_p", align_bytes=64)
        xs_p = keep.tile([P, KG * P], U8, name="xs_p", align_bytes=64)
        nc.vector.quantize_mx(
            out=xc_p[:].bitcast(FP8X4), scales=xs_p[:], in_=grouped_p[:].rearrange("p g n t -> p (g n t)")
        )
        for table, mine, op in ((i_wm, pw, ALU.is_le), (i_hp, ph, ALU.is_ge), (i_hm, ph, ALU.is_le)):
            nc.vector.scalar_tensor_tensor(
                out=band[:], in0=table[:], scalar=mine[:], in1=band[:], op0=op, op1=ALU.mult
            )

        q_sb = keep.tile([P, 16, P], F32, name="q_sb")
        v_sb = keep.tile([P, CO], F32, name="v_sb")
        o_sb = keep.tile([P, 16, P], F32, name="o_sb")
        pt = keep.tile([P, 8, P], F32, name="pt")
        ca = keep.tile([P, 8, 4, 4], F32, name="ca")
        pd = keep.tile([P, 8, 16, 8], F32, name="pd")
        a_sb = keep.tile([P, 8, 3, 3], F32, name="a_sb")
        out_view = out_0[0].rearrange("(m p) h w -> p m (h w)", p=P)
        live = {}

        def rel_mm():
            rel_ps = ps_tr.tile([P, 3, P], F32, tag="tr")
            for n in range(3):
                nc.tensor.transpose(out=rel_ps[:, n, :], in_=zc[:, n, :], identity=ident[:])
            live["rel"] = rel_ps

        def rel_cp():
            nc.vector.tensor_copy(out=kr[:, :, P : P + 3], in_=live["rel"][:, :, 0:16].rearrange("p n m -> p m n"))

        def project(words, s, c, codes, code_scales):
            acc = ps_acc.tile([P, 4, P], F32, tag="acc")
            for j in range(4):
                cols = slice(P * (4 * c + j), P * (4 * c + j + 1))
                for g in range(KG):
                    nc.tensor.matmul_mx(
                        out=acc[:, j, :],
                        lhsT=words[:, g, cols].bitcast(FP8X4),
                        lhsT_scale=planes[4 * g : P, s, cols],
                        rhs=codes[:, P * g : P * (g + 1)].bitcast(FP8X4),
                        rhs_scale=code_scales[:, P * g : P * (g + 1)],
                        start=(g == 0),
                        stop=(g == KG - 1),
                    )
            return acc

        def q_mm(c):
            live["q", c] = project(wq, 0, c, xc, xs)

        def q_cp(c):
            nc.scalar.copy(out=q_sb[:, 4 * c : 4 * c + 4, :], in_=live["q", c][:])

        def k_banks(c):
            ka = ps_acc.tile([P, 2, P], F32, tag="acc")
            kb = ps_pv.tile([P, 2, P], F32, tag="pv")
            live["k", c] = (ka, kb)

        def k_pass(c, j, g, start, stop):
            cols = slice(P * (4 * c + j), P * (4 * c + j + 1))
            nc.tensor.matmul_mx(
                out=live["k", c][j // 2][:, j % 2, :],
                lhsT=wk[:, g, cols].bitcast(FP8X4),
                lhsT_scale=planes[4 * g : P, 1, cols],
                rhs=xc_p[:, P * g : P * (g + 1)].bitcast(FP8X4),
                rhs_scale=xs_p[:, P * g : P * (g + 1)],
                start=start,
                stop=stop,
            )

        def k_mm(c):
            k_banks(c)
            for j in range(4):
                for g in range(KG):
                    k_pass(c, j, g, g == 0, g == KG - 1)

        def kk_mm(g):
            if g == 0:
                k_banks(3)
            for j in range(4):
                k_pass(3, j, g, g == 0 and j % 2 == 0, g == KG - 1 and j % 2 == 1)

        def k_cp(c):
            nc.scalar.copy(out=kr[:, 4 * c : 4 * c + 2, 0:P], in_=live["k", c][0][:])
            nc.vector.tensor_copy(out=kr[:, 4 * c + 2 : 4 * c + 4, 0:P], in_=live["k", c][1][:])

        def s_mm(c):
            s_ps = ps_s.tile([P, 2, P + 4], F32, tag="s")
            for gl in range(2):
                for s2 in range(2):
                    m = 4 * c + 2 * gl + s2
                    nc.tensor.matmul(
                        out=s_ps[:, gl, :], lhsT=q_sb[:, m, :], rhs=kr[:, m, 0 : P + 4], start=(s2 == 0), stop=(s2 == 1)
                    )
            live["s", c] = s_ps

        def mask(c):
            sm = work.tile([P, 2, 16, 8], F32, tag="sm")
            nc.vector.tensor_tensor(
                out=sm[:].rearrange("p g c r -> p g (c r)"),
                in0=live["s", c][:, :, 0:P],
                in1=band[:].unsqueeze(1).to_broadcast([P, 2, P]),
                op=ALU.mult,
            )
            live["sm", c] = sm

        def rsel(c):
            picked = work.tile([P, 2, 4, 4], F32, tag="picked")
            nc.vector.tensor_tensor(
                out=picked[:],
                in0=live["s", c][:, :, P : P + 4].unsqueeze(2).to_broadcast([P, 2, 4, 4]),
                in1=(sel_h if c < 2 else sel_w)[:].unsqueeze(1).to_broadcast([P, 2, 4, 4]),
                op=ALU.mult,
            )
            live["picked", c] = picked

        def red(c):
            e = work.tile([P, 2, 16], F32, tag="e")
            nc.vector.tensor_reduce(out=e[:], in_=live["sm", c][:], axis=AX.X, op=ALU.add)
            live["e", c] = e

        def rc(c):
            r_cls = work.tile([P, 2, 4], F32, tag="r_cls")
            nc.vector.tensor_reduce(out=r_cls[:], in_=live["picked", c][:], axis=AX.X, op=ALU.add)
            live["r_cls", c] = r_cls

        def rv(c):
            r_all = work.tile([P, 2, 4, 4], F32, tag="r_all")
            nc.vector.tensor_tensor(
                out=r_all[:],
                in0=vm[:].unsqueeze(1).to_broadcast([P, 2, 4, 4]),
                in1=live["r_cls", c][:].unsqueeze(3 if c < 2 else 2).to_broadcast([P, 2, 4, 4]),
                op=ALU.add,
            )
            live["r_all", c] = r_all

        def eadd(c):
            e = live["e", c]
            nc.vector.tensor_tensor(
                out=e[:], in0=e[:], in1=live["r_all", c][:].rearrange("p g a b -> p g (a b)"), op=ALU.add
            )

        def negmx(c):
            neg_max = work.tile([P, 2], F32, tag="neg_max")
            nc.vector.tensor_reduce(out=neg_max[:], in_=live["e", c][:], axis=AX.X, op=ALU.max, negate=True)
            live["neg_max", c] = neg_max

        def exp(c):
            e = live["e", c]
            den = work.tile([P, 2], F32, tag="den")
            for gl in range(2):
                nc.scalar.activation(
                    out=e[:, gl, :],
                    in_=e[:, gl, :],
                    func=ACT.Exp,
                    bias=live["neg_max", c][:, gl : gl + 1],
                    scale=1.0,
                    accum_out=den[:, gl : gl + 1],
                )
            live["den", c] = den

        def recip(c):
            nc.vector.reciprocal(out=live["den", c][:], in_=live["den", c][:])

        def canorm(c):
            nc.vector.tensor_tensor(
                out=ca[:, 2 * c : 2 * c + 2].rearrange("p g a b -> p g (a b)"),
                in0=live["e", c][:],
                in1=live["den", c][:].unsqueeze(2).to_broadcast([P, 2, 16]),
                op=ALU.mult,
            )

        def pdense(c):
            nc.vector.tensor_tensor(
                out=pd[:, 2 * c : 2 * c + 2],
                in0=ca[:, 2 * c : 2 * c + 2].rearrange("p g a b -> p g (a b)").unsqueeze(3).to_broadcast([P, 2, 16, 8]),
                in1=band[:].rearrange("p (c r) -> p c r", r=8).unsqueeze(1).to_broadcast([P, 2, 16, 8]),
                op=ALU.mult,
            )

        def t_mm(c):
            tr_ps = ps_tr.tile([P, 2, P], F32, tag="tr")
            for gl in range(2):
                nc.tensor.transpose(
                    out=tr_ps[:, gl, :], in_=pd[:, 2 * c + gl].rearrange("p c r -> p (c r)"), identity=ident[:]
                )
            live["tr", c] = tr_ps

        def t_cp(c):
            nc.scalar.copy(out=pt[:, 2 * c : 2 * c + 2, :], in_=live["tr", c][:])

        def v_mm(i):
            m0, n_tiles = V_CHUNKS[i]
            vacc = ps_acc.tile([P, P * n_tiles], F32, tag="acc")
            cols = slice(P * m0, P * (m0 + n_tiles))
            for g in range(KG):
                nc.tensor.matmul_mx(
                    out=vacc[:],
                    lhsT=xc_p[:, P * g : P * (g + 1)].bitcast(FP8X4),
                    lhsT_scale=xs_p[:, P * g : P * (g + 1)],
                    rhs=wv[:, g, cols].bitcast(FP8X4),
                    rhs_scale=planes[4 * g : P, 2, cols],
                    start=(g == 0),
                    stop=(g == KG - 1),
                )
            live["v", i] = vacc

        def vv_mm(g):
            for i in (3, 4):
                m0, n_tiles = V_CHUNKS[i]
                if g == 0:
                    vacc = ps_s.tile([P, P * n_tiles], F32, tag="s")
                    live["v", i] = vacc
                cols = slice(P * m0, P * (m0 + n_tiles))
                nc.tensor.matmul_mx(
                    out=live["v", i][:],
                    lhsT=xc_p[:, P * g : P * (g + 1)].bitcast(FP8X4),
                    lhsT_scale=xs_p[:, P * g : P * (g + 1)],
                    rhs=wv[:, g, cols].bitcast(FP8X4),
                    rhs_scale=planes[4 * g : P, 2, cols],
                    start=(g == 0),
                    stop=(g == KG - 1),
                )

        def v_cp(i):
            m0, n_tiles = V_CHUNKS[i]
            if i == 4:
                nc.vector.tensor_copy(out=v_sb[:, P * m0 : P * (m0 + n_tiles)], in_=live["v", i][:])
            else:
                nc.scalar.copy(out=v_sb[:, P * m0 : P * (m0 + n_tiles)], in_=live["v", i][:])

        def p_mm(i):
            m0, n_tiles = V_CHUNKS[i]
            if i == 4:
                pv = ps_tr.tile([P, n_tiles, P], F32, tag="tr")
            else:
                pv = ps_pv.tile([P, n_tiles, P], F32, tag="pv")
            for j in range(n_tiles):
                m = m0 + j
                nc.tensor.matmul(
                    out=pv[:, j, :], lhsT=v_sb[:, P * m : P * (m + 1)], rhs=pt[:, m // 2, :], start=True, stop=True
                )
            live["pv", i] = pv

        def o_cp(i):
            m0, n_tiles = V_CHUNKS[i]
            if i == 3:
                nc.scalar.copy(out=o_sb[:, m0 : m0 + n_tiles, :], in_=live["pv", i][:])
            else:
                nc.vector.tensor_copy(out=o_sb[:, m0 : m0 + n_tiles, :], in_=live["pv", i][:])
            nc.sync.dma_start(out=out_view[:, m0 : m0 + n_tiles, :], in_=o_sb[:, m0 : m0 + n_tiles, :])

        def w1_(half):
            by_a = work.tile([P, 4, 3, 4, 4], F32, tag="by_a")
            for i in range(3):
                nc.vector.tensor_tensor(
                    out=by_a[:, :, i],
                    in0=ca[:, 4 * half : 4 * half + 4].rearrange("p g a b -> p g b a"),
                    in1=sel_h[:, :, i].unsqueeze(1).unsqueeze(1).to_broadcast([P, 4, 4, 4]),
                    op=ALU.mult,
                )
            live["by_a", half] = by_a

        def w2_(half):
            rows = work.tile([P, 12, 4], F32, tag="rows")
            nc.vector.tensor_reduce(
                out=rows[:].rearrange("p r b -> p (r b)"),
                in_=live["by_a", half][:].rearrange("p g i b a -> p (g i b) a"),
                axis=AX.X,
                op=ALU.add,
            )
            live["rows", half] = rows

        def w3_(half):
            by_b = work.tile([P, 12, 3, 4], F32, tag="by_b")
            nc.vector.tensor_tensor(
                out=by_b[:],
                in0=live["rows", half][:].unsqueeze(2).to_broadcast([P, 12, 3, 4]),
                in1=sel_w[:, :, 0:3].rearrange("p b j -> p j b").unsqueeze(1).to_broadcast([P, 12, 3, 4]),
                op=ALU.mult,
            )
            live["by_b", half] = by_b

        def w4_(half):
            g0 = 4 * half
            nc.vector.tensor_reduce(
                out=a_sb[:, g0 : g0 + 4].rearrange("p g i j -> p (g i j)"),
                in_=live["by_b", half][:].rearrange("p r j b -> p (r j) b"),
                axis=AX.X,
                op=ALU.add,
            )
            nc.sync.dma_start(
                out=out_1[0, g0 : g0 + 4].rearrange("g h w n -> (h w) g n"),
                in_=a_sb[:, g0 : g0 + 4].rearrange("p g i j -> p g (i j)"),
            )

        rel_mm()
        rel_cp()
        q_mm(0)
        q_cp(0)
        k_mm(0)
        k_cp(0)
        s_mm(0)
        mask(0)
        rsel(0)
        red(0)
        rc(0)
        rv(0)
        eadd(0)
        negmx(0)
        q_mm(1)
        q_cp(1)
        exp(0)
        k_mm(1)
        k_cp(1)
        s_mm(1)
        recip(0)
        canorm(0)
        pdense(0)
        mask(1)
        rsel(1)
        red(1)
        rc(1)
        rv(1)
        eadd(1)
        negmx(1)
        q_mm(2)
        q_cp(2)
        exp(1)
        k_mm(2)
        k_cp(2)
        t_mm(0)
        t_cp(0)
        s_mm(2)
        recip(1)
        canorm(1)
        pdense(1)
        w1_(0)
        w2_(0)
        mask(2)
        rsel(2)
        w3_(0)
        red(2)
        rc(2)
        w4_(0)
        rv(2)
        eadd(2)
        negmx(2)
        q_mm(3)
        q_cp(3)
        exp(2)
        kk_mm(0)
        kk_mm(1)
        kk_mm(2)
        kk_mm(3)
        k_cp(3)
        t_mm(1)
        t_cp(1)
        s_mm(3)
        recip(2)
        canorm(2)
        pdense(2)
        mask(3)
        rsel(3)
        red(3)
        rc(3)
        rv(3)
        eadd(3)
        negmx(3)
        v_mm(0)
        v_cp(0)
        exp(3)
        v_mm(1)
        v_cp(1)
        t_mm(2)
        t_cp(2)
        p_mm(0)
        recip(3)
        canorm(3)
        pdense(3)
        w1_(1)
        w2_(1)
        w3_(1)
        w4_(1)
        o_cp(0)
        p_mm(1)
        o_cp(1)
        v_mm(2)
        v_cp(2)
        vv_mm(0)
        vv_mm(1)
        vv_mm(2)
        t_mm(3)
        t_cp(3)
        vv_mm(3)
        v_cp(3)
        v_cp(4)
        p_mm(2)
        p_mm(3)
        o_cp(2)
        p_mm(4)
        o_cp(3)
        o_cp(4)
